import numpy as np
import ml_dtypes

BF16 = ml_dtypes.bfloat16


def bf(x):
    return np.asarray(x, np.float32).astype(BF16)


def f32(x):
    return np.asarray(x, np.float32)


def f64(x):
    return np.asarray(x).astype(np.float64)


def striped(idx):
    return np.tile(idx.reshape(-1, 16).T, (8, 1))


C, S, N, M = 512, 256, 128, 1536


def sigmoid(v):
    return 1.0 / (1.0 + np.exp(-v))


def setup_inputs():
    return {
        "base": f32(np.random.standard_normal((C, S))),
        "msg": bf(np.random.standard_normal((C, N))),
        "h": bf(np.random.standard_normal((C, N))),
        "w_i": bf(np.random.standard_normal((C, M)) / np.sqrt(C)),
        "w_h": bf(np.random.standard_normal((C, M)) / np.sqrt(C)),
        "b_i": f32(0.5 * np.random.standard_normal((M, 1))),
        "b_hn": f32(0.5 * np.random.standard_normal((C, 1))),
        "offs": striped(np.random.permutation(S)[:N]),
    }


def reference(base, msg, h, w_i, w_h, b_i, b_hn, offs):
    idx = offs[:16].T.reshape(-1)
    i_r, i_z, i_n = np.split(f64(w_i).T @ f64(msg) + f64(b_i), M // C)
    h_r, h_z, h_n = np.split(f64(w_h).T @ f64(h), M // C)
    r = sigmoid(i_r + h_r)
    z = sigmoid(i_z + h_z)
    n = np.tanh(i_n + r * (h_n + f64(b_hn)))
    out = f64(base).copy()
    out[:, idx] = (1.0 - z) * n + z * f64(h)
    return out

@@ -1,0 +1,114 @@
+import concourse.masks as masks
+import concourse.mybir as mybir
+
+F32 = mybir.dt.float32
+BF16 = mybir.dt.bfloat16
+U16 = mybir.dt.uint16
+ADD = mybir.AluOpType.add
+MULT = mybir.AluOpType.mult
+SIGMOID = mybir.ActivationFunctionType.Sigmoid
+TANH = mybir.ActivationFunctionType.Tanh
+
+P = 128
+C = 512
+N = 128
+S = 256
+BLOCKS = C // P
+
+RESET, UPDATE, CANDIDATE = 0, 1, 2
+
+FLOPS = 2 * 2 * C * 3 * C * N
+
+
+def tile_graphconvolutionlayer_kernel(tc, base, msg, h, w_i, w_h, b_i, b_hn, offs, out):
+    nc = tc.nc
+    with (
+        tc.tile_pool(name="held", bufs=1) as held,
+        tc.psum_pool(name="banks", bufs=8) as banks,
+    ):
+        offsets = held.tile([P, N // 16], U16, name="offsets")
+        nc.sync.dma_start(offsets[:], offs)
+
+        msg_sb = held.tile([P, BLOCKS, N], BF16, name="msg_sb")
+        nc.sync.dma_start(msg_sb[:], msg.rearrange("(kb p) j -> p kb j", p=P))
+        h_sb = held.tile([P, BLOCKS, N], BF16, name="h_sb")
+        nc.scalar.dma_start(h_sb[:], h.rearrange("(kb p) j -> p kb j", p=P))
+
+        w_i_sb = {}
+        w_h_sb = {}
+        for gate in (RESET, CANDIDATE, UPDATE):
+            columns = slice(gate * C, (gate + 1) * C)
+            w_i_sb[gate] = held.tile([P, BLOCKS, C], BF16, name=f"w_i_sb{gate}")
+            nc.sync.dma_start(w_i_sb[gate][:], w_i.rearrange("(kb p) m -> p kb m", p=P)[:, :, columns])
+            w_h_sb[gate] = held.tile([P, BLOCKS, C], BF16, name=f"w_h_sb{gate}")
+            nc.scalar.dma_start(w_h_sb[gate][:], w_h.rearrange("(kb p) m -> p kb m", p=P)[:, :, columns])
+
+        windows = []
+        for cb in range(BLOCKS):
+            window = held.tile([P, S], F32, name=f"window{cb}")
+            queue = nc.sync if cb % 2 == 0 else nc.scalar
+            queue.dma_start(window[:], base[cb * P : (cb + 1) * P, :])
+            windows.append(window)
+
+        identity = held.tile([P, P], F32, name="identity")
+        masks.make_identity(nc, identity[:])
+        bias_rows = held.tile([P, P], F32, name="bias_rows")
+        nc.gpsimd.memset(bias_rows[:], 0.0)
+        nc.gpsimd.dma_start(bias_rows[0 : 3 * BLOCKS, :], b_i.rearrange("(n p) o -> n (p o)", p=P))
+        nc.gpsimd.dma_start(bias_rows[3 * BLOCKS : 4 * BLOCKS, :], b_hn.rearrange("(n p) o -> n (p o)", p=P))
+        bias_ps = banks.tile([P, P], F32, name="bias_ps", tag="bank")
+        nc.tensor.transpose(bias_ps[:], bias_rows[:], identity[:])
+        bias = held.tile([P, 4 * BLOCKS], F32, name="bias")
+        nc.vector.tensor_copy(bias[:], bias_ps[:, 0 : 4 * BLOCKS])
+
+        def b_i_column(gate, cb):
+            return bias[:, gate * BLOCKS + cb : gate * BLOCKS + cb + 1]
+
+        def b_hn_column(cb):
+            return bias[:, 3 * BLOCKS + cb : 3 * BLOCKS + cb + 1]
+
+        def multiply(bank, w_sb, cb, moving, start, stop):
+            for kb in range(BLOCKS):
+                nc.tensor.matmul(
+                    bank[:],
+                    lhsT=w_sb[:, kb, cb * P : (cb + 1) * P],
+                    rhs=moving[:, kb, :],
+                    start=start and kb == 0,
+                    stop=stop and kb == BLOCKS - 1,
+                )
+
+        r = []
+        sum_r = [banks.tile([P, N], F32, name=f"sum_r{cb}", tag="bank") for cb in range(BLOCKS)]
+        for cb in range(BLOCKS):
+            multiply(sum_r[cb], w_i_sb[RESET], cb, msg_sb, start=True, stop=False)
+        for cb in range(BLOCKS):
+            multiply(sum_r[cb], w_h_sb[RESET], cb, h_sb, start=False, stop=True)
+            r.append(held.tile([P, N], F32, name=f"r{cb}"))
+            nc.scalar.activation(r[cb][:], sum_r[cb][:], SIGMOID, bias=b_i_column(RESET, cb))
+
+        n = []
+        for cb in range(BLOCKS):
+            e_n = banks.tile([P, N], F32, name=f"e_n{cb}", tag="bank")
+            multiply(e_n, w_h_sb[CANDIDATE], cb, h_sb, start=True, stop=True)
+            a_n = banks.tile([P, N], F32, name=f"a_n{cb}", tag="bank")
+            multiply(a_n, w_i_sb[CANDIDATE], cb, msg_sb, start=True, stop=True)
+            gated = held.tile([P, N], F32, name=f"gated{cb}")
+            nc.vector.scalar_tensor_tensor(gated[:], e_n[:], b_hn_column(cb), r[cb][:], op0=ADD, op1=MULT)
+            nc.vector.tensor_tensor(gated[:], gated[:], a_n[:], ADD)
+            n.append(held.tile([P, N], F32, name=f"n{cb}"))
+            nc.scalar.activation(n[cb][:], gated[:], TANH, bias=b_i_column(CANDIDATE, cb))
+
+        sum_z = [banks.tile([P, N], F32, name=f"sum_z{cb}", tag="bank") for cb in range(BLOCKS)]
+        for cb in range(BLOCKS):
+            multiply(sum_z[cb], w_i_sb[UPDATE], cb, msg_sb, start=True, stop=False)
+        for cb in range(BLOCKS):
+            multiply(sum_z[cb], w_h_sb[UPDATE], cb, h_sb, start=False, stop=True)
+            z = held.tile([P, N], F32, name=f"z{cb}")
+            nc.scalar.activation(z[:], sum_z[cb][:], SIGMOID, bias=b_i_column(UPDATE, cb))
+            kept = held.tile([P, N], F32, name=f"kept{cb}")
+            nc.vector.tensor_tensor(kept[:], z[:], h_sb[:, cb, :], MULT)
+            fresh = held.tile([P, N], F32, name=f"fresh{cb}")
+            nc.vector.tensor_scalar(fresh[:], z[:], -1.0, 1.0, op0=MULT, op1=ADD)
+            nc.vector.tensor_tensor(fresh[:], fresh[:], n[cb][:], MULT)
+            nc.vector.tensor_tensor(windows[cb][:].indirect(offsets[:]), fresh[:], kept[:], ADD)
+            nc.sync.dma_start(out[cb * P : (cb + 1) * P, :], windows[cb][:])

@@ -28,34 +28,40 @@ def tile_graphconvolutionlayer_kernel(tc, base, msg, h, w_i, w_h, b_i, b_hn, off
     ):
         offsets = held.tile([P, N // 16], U16, name="offsets")
         nc.sync.dma_start(offsets[:], offs)
-
         msg_sb = held.tile([P, BLOCKS, N], BF16, name="msg_sb")
         nc.sync.dma_start(msg_sb[:], msg.rearrange("(kb p) j -> p kb j", p=P))
         h_sb = held.tile([P, BLOCKS, N], BF16, name="h_sb")
         nc.scalar.dma_start(h_sb[:], h.rearrange("(kb p) j -> p kb j", p=P))
 
-        w_i_sb = {}
-        w_h_sb = {}
-        for gate in (RESET, CANDIDATE, UPDATE):
-            columns = slice(gate * C, (gate + 1) * C)
-            w_i_sb[gate] = held.tile([P, BLOCKS, C], BF16, name=f"w_i_sb{gate}")
-            nc.sync.dma_start(w_i_sb[gate][:], w_i.rearrange("(kb p) m -> p kb m", p=P)[:, :, columns])
-            w_h_sb[gate] = held.tile([P, BLOCKS, C], BF16, name=f"w_h_sb{gate}")
-            nc.scalar.dma_start(w_h_sb[gate][:], w_h.rearrange("(kb p) m -> p kb m", p=P)[:, :, columns])
+        bias_rows = held.tile([P, P], F32, name="bias_rows")
+        nc.vector.memset(bias_rows[:], 0.0)
+        nc.scalar.dma_start(bias_rows[0 : 3 * BLOCKS, :], b_i.rearrange("(n p) o -> n (p o)", p=P))
+        nc.scalar.dma_start(bias_rows[3 * BLOCKS : 4 * BLOCKS, :], b_hn.rearrange("(n p) o -> n (p o)", p=P))
 
+        w_i_rz = []
+        w_h_rz = []
+        for kb in range(BLOCKS):
+            rows = slice(kb * P, (kb + 1) * P)
+            w_i_rz.append(held.tile([P, 2 * C], BF16, name=f"w_i_rz{kb}"))
+            nc.sync.dma_start(w_i_rz[kb][:], w_i[rows, 0 : 2 * C])
+            w_h_rz.append(held.tile([P, 2 * C], BF16, name=f"w_h_rz{kb}"))
+            nc.sync.dma_start(w_h_rz[kb][:], w_h[rows, 0 : 2 * C])
+        w_h_n = []
+        for kb in range(BLOCKS):
+            w_h_n.append(held.tile([P, C], BF16, name=f"w_h_n{kb}"))
+            nc.sync.dma_start(w_h_n[kb][:], w_h[kb * P : (kb + 1) * P, 2 * C : 3 * C])
+        w_i_n = []
         windows = []
-        for cb in range(BLOCKS):
-            window = held.tile([P, S], F32, name=f"window{cb}")
-            queue = nc.sync if cb % 2 == 0 else nc.scalar
-            queue.dma_start(window[:], base[cb * P : (cb + 1) * P, :])
-            windows.append(window)
+        for half in range(2):
+            columns = slice(2 * C + half * 2 * P, 2 * C + (half + 1) * 2 * P)
+            w_i_n.append(held.tile([P, BLOCKS, 2 * P], BF16, name=f"w_i_n{half}"))
+            nc.sync.dma_start(w_i_n[half][:], w_i.rearrange("(kb p) m -> p kb m", p=P)[:, :, columns])
+            for cb in (2 * half, 2 * half + 1):
+                windows.append(held.tile([P, S], F32, name=f"window{cb}"))
+                nc.sync.dma_start(windows[cb][:], base[cb * P : (cb + 1) * P, :])
 
         identity = held.tile([P, P], F32, name="identity")
         masks.make_identity(nc, identity[:])
-        bias_rows = held.tile([P, P], F32, name="bias_rows")
-        nc.gpsimd.memset(bias_rows[:], 0.0)
-        nc.gpsimd.dma_start(bias_rows[0 : 3 * BLOCKS, :], b_i.rearrange("(n p) o -> n (p o)", p=P))
-        nc.gpsimd.dma_start(bias_rows[3 * BLOCKS : 4 * BLOCKS, :], b_hn.rearrange("(n p) o -> n (p o)", p=P))
         bias_ps = banks.tile([P, P], F32, name="bias_ps", tag="bank")
         nc.tensor.transpose(bias_ps[:], bias_rows[:], identity[:])
         bias = held.tile([P, 4 * BLOCKS], F32, name="bias")
@@ -67,48 +73,58 @@ def tile_graphconvolutionlayer_kernel(tc, base, msg, h, w_i, w_h, b_i, b_hn, off
         def b_hn_column(cb):
             return bias[:, 3 * BLOCKS + cb : 3 * BLOCKS + cb + 1]
 
-        def multiply(bank, w_sb, cb, moving, start, stop):
+        sum_r = [banks.tile([P, N], F32, name=f"sum_r{cb}", tag="bank") for cb in range(BLOCKS)]
+        sum_z = [banks.tile([P, N], F32, name=f"sum_z{cb}", tag="bank") for cb in range(BLOCKS)]
+        for kb in range(BLOCKS):
+            for w_sb, moving, first, last in ((w_i_rz[kb], msg_sb, kb == 0, False), (w_h_rz[kb], h_sb, False, kb == BLOCKS - 1)):
+                for gate, sums in ((RESET, sum_r), (UPDATE, sum_z)):
+                    for cb in range(BLOCKS):
+                        nc.tensor.matmul(
+                            sums[cb][:],
+                            lhsT=w_sb[:, gate * C + cb * P : gate * C + (cb + 1) * P],
+                            rhs=moving[:, kb, :],
+                            start=first,
+                            stop=last,
+                        )
+        r = held.tile([P, BLOCKS, N], F32, name="r")
+        z = held.tile([P, BLOCKS, N], F32, name="z")
+        for cb in range(BLOCKS):
+            nc.scalar.activation(r[:, cb, :], sum_r[cb][:], SIGMOID, bias=b_i_column(RESET, cb))
+        for cb in range(BLOCKS):
+            nc.scalar.activation(z[:, cb, :], sum_z[cb][:], SIGMOID, bias=b_i_column(UPDATE, cb))
+        kept = held.tile([P, BLOCKS, N], F32, name="kept")
+        nc.vector.tensor_tensor(kept[:], z[:], h_sb[:], MULT)
+        one_minus_z = held.tile([P, BLOCKS, N], F32, name="one_minus_z")
+        nc.vector.tensor_scalar(one_minus_z[:], z[:], -1.0, 1.0, op0=MULT, op1=ADD)
+
+        e_n = [banks.tile([P, N], F32, name=f"e_n{cb}", tag="bank") for cb in range(BLOCKS)]
+        for kb in range(BLOCKS):
+            for cb in range(BLOCKS):
+                nc.tensor.matmul(
+                    e_n[cb][:],
+                    lhsT=w_h_n[kb][:, cb * P : (cb + 1) * P],
+                    rhs=h_sb[:, kb, :],
+                    start=kb == 0,
+                    stop=kb == BLOCKS - 1,
+                )
+        gated = held.tile([P, BLOCKS, N], F32, name="gated")
+        for cb in range(BLOCKS):
+            nc.vector.scalar_tensor_tensor(gated[:, cb, :], e_n[cb][:], b_hn_column(cb), r[:, cb, :], op0=ADD, op1=MULT)
+
+        for cb in range(BLOCKS):
+            a_n = banks.tile([P, N], F32, name=f"a_n{cb}", tag="bank")
             for kb in range(BLOCKS):
                 nc.tensor.matmul(
-                    bank[:],
-                    lhsT=w_sb[:, kb, cb * P : (cb + 1) * P],
-                    rhs=moving[:, kb, :],
-                    start=start and kb == 0,
-                    stop=stop and kb == BLOCKS - 1,
+                    a_n[:],
+                    lhsT=w_i_n[cb // 2][:, kb, (cb % 2) * P : (cb % 2 + 1) * P],
+                    rhs=msg_sb[:, kb, :],
+                    start=kb == 0,
+                    stop=kb == BLOCKS - 1,
                 )
-
-        r = []
-        sum_r = [banks.tile([P, N], F32, name=f"sum_r{cb}", tag="bank") for cb in range(BLOCKS)]
-        for cb in range(BLOCKS):
-            multiply(sum_r[cb], w_i_sb[RESET], cb, msg_sb, start=True, stop=False)
-        for cb in range(BLOCKS):
-            multiply(sum_r[cb], w_h_sb[RESET], cb, h_sb, start=False, stop=True)
-            r.append(held.tile([P, N], F32, name=f"r{cb}"))
-            nc.scalar.activation(r[cb][:], sum_r[cb][:], SIGMOID, bias=b_i_column(RESET, cb))
-
-        n = []
-        for cb in range(BLOCKS):
-            e_n = banks.tile([P, N], F32, name=f"e_n{cb}", tag="bank")
-            multiply(e_n, w_h_sb[CANDIDATE], cb, h_sb, start=True, stop=True)
-            a_n = banks.tile([P, N], F32, name=f"a_n{cb}", tag="bank")
-            multiply(a_n, w_i_sb[CANDIDATE], cb, msg_sb, start=True, stop=True)
-            gated = held.tile([P, N], F32, name=f"gated{cb}")
-            nc.vector.scalar_tensor_tensor(gated[:], e_n[:], b_hn_column(cb), r[cb][:], op0=ADD, op1=MULT)
-            nc.vector.tensor_tensor(gated[:], gated[:], a_n[:], ADD)
-            n.append(held.tile([P, N], F32, name=f"n{cb}"))
-            nc.scalar.activation(n[cb][:], gated[:], TANH, bias=b_i_column(CANDIDATE, cb))
-
-        sum_z = [banks.tile([P, N], F32, name=f"sum_z{cb}", tag="bank") for cb in range(BLOCKS)]
-        for cb in range(BLOCKS):
-            multiply(sum_z[cb], w_i_sb[UPDATE], cb, msg_sb, start=True, stop=False)
-        for cb in range(BLOCKS):
-            multiply(sum_z[cb], w_h_sb[UPDATE], cb, h_sb, start=False, stop=True)
-            z = held.tile([P, N], F32, name=f"z{cb}")
-            nc.scalar.activation(z[:], sum_z[cb][:], SIGMOID, bias=b_i_column(UPDATE, cb))
-            kept = held.tile([P, N], F32, name=f"kept{cb}")
-            nc.vector.tensor_tensor(kept[:], z[:], h_sb[:, cb, :], MULT)
+            n = held.tile([P, N], F32, name=f"n{cb}")
+            nc.vector.tensor_tensor(n[:], gated[:, cb, :], a_n[:], ADD)
+            nc.scalar.activation(n[:], n[:], TANH, bias=b_i_column(CANDIDATE, cb))
             fresh = held.tile([P, N], F32, name=f"fresh{cb}")
-            nc.vector.tensor_scalar(fresh[:], z[:], -1.0, 1.0, op0=MULT, op1=ADD)
-            nc.vector.tensor_tensor(fresh[:], fresh[:], n[cb][:], MULT)
-            nc.vector.tensor_tensor(windows[cb][:].indirect(offsets[:]), fresh[:], kept[:], ADD)
+            nc.vector.tensor_tensor(fresh[:], one_minus_z[:, cb, :], n[:], MULT)
+            nc.vector.tensor_tensor(windows[cb][:].indirect(offsets[:]), fresh[:], kept[:, cb, :], ADD)
             nc.sync.dma_start(out[cb * P : (cb + 1) * P, :], windows[cb][:])

@@ -45,11 +45,11 @@ def tile_graphconvolutionlayer_kernel(tc, base, msg, h, w_i, w_h, b_i, b_hn, off
             w_i_rz.append(held.tile([P, 2 * C], BF16, name=f"w_i_rz{kb}"))
             nc.sync.dma_start(w_i_rz[kb][:], w_i[rows, 0 : 2 * C])
             w_h_rz.append(held.tile([P, 2 * C], BF16, name=f"w_h_rz{kb}"))
-            nc.sync.dma_start(w_h_rz[kb][:], w_h[rows, 0 : 2 * C])
+            nc.scalar.dma_start(w_h_rz[kb][:], w_h[rows, 0 : 2 * C])
         w_h_n = []
         for kb in range(BLOCKS):
             w_h_n.append(held.tile([P, C], BF16, name=f"w_h_n{kb}"))
-            nc.sync.dma_start(w_h_n[kb][:], w_h[kb * P : (kb + 1) * P, 2 * C : 3 * C])
+            nc.scalar.dma_start(w_h_n[kb][:], w_h[kb * P : (kb + 1) * P, 2 * C : 3 * C])
         w_i_n = []
         windows = []
         for half in range(2):

@@ -38,27 +38,21 @@ def tile_graphconvolutionlayer_kernel(tc, base, msg, h, w_i, w_h, b_i, b_hn, off
         nc.scalar.dma_start(bias_rows[0 : 3 * BLOCKS, :], b_i.rearrange("(n p) o -> n (p o)", p=P))
         nc.scalar.dma_start(bias_rows[3 * BLOCKS : 4 * BLOCKS, :], b_hn.rearrange("(n p) o -> n (p o)", p=P))
 
-        w_i_rz = []
-        w_h_rz = []
-        for kb in range(BLOCKS):
-            rows = slice(kb * P, (kb + 1) * P)
-            w_i_rz.append(held.tile([P, 2 * C], BF16, name=f"w_i_rz{kb}"))
-            nc.sync.dma_start(w_i_rz[kb][:], w_i[rows, 0 : 2 * C])
-            w_h_rz.append(held.tile([P, 2 * C], BF16, name=f"w_h_rz{kb}"))
-            nc.scalar.dma_start(w_h_rz[kb][:], w_h[rows, 0 : 2 * C])
-        w_h_n = []
-        for kb in range(BLOCKS):
-            w_h_n.append(held.tile([P, C], BF16, name=f"w_h_n{kb}"))
-            nc.scalar.dma_start(w_h_n[kb][:], w_h[kb * P : (kb + 1) * P, 2 * C : 3 * C])
-        w_i_n = []
+        w_i_sb = {}
+        w_h_sb = {}
+        for gate in (RESET, CANDIDATE, UPDATE):
+            for kb in range(BLOCKS):
+                rows = slice(kb * P, (kb + 1) * P)
+                columns = slice(gate * C, (gate + 1) * C)
+                w_i_sb[gate, kb] = held.tile([P, C], BF16, name=f"w_i_sb{gate}_{kb}")
+                nc.sync.dma_start(w_i_sb[gate, kb][:], w_i[rows, columns])
+                w_h_sb[gate, kb] = held.tile([P, C], BF16, name=f"w_h_sb{gate}_{kb}")
+                nc.sync.dma_start(w_h_sb[gate, kb][:], w_h[rows, columns])
+
         windows = []
-        for half in range(2):
-            columns = slice(2 * C + half * 2 * P, 2 * C + (half + 1) * 2 * P)
-            w_i_n.append(held.tile([P, BLOCKS, 2 * P], BF16, name=f"w_i_n{half}"))
-            nc.sync.dma_start(w_i_n[half][:], w_i.rearrange("(kb p) m -> p kb m", p=P)[:, :, columns])
-            for cb in (2 * half, 2 * half + 1):
-                windows.append(held.tile([P, S], F32, name=f"window{cb}"))
-                nc.sync.dma_start(windows[cb][:], base[cb * P : (cb + 1) * P, :])
+        for cb in range(BLOCKS):
+            windows.append(held.tile([P, S], F32, name=f"window{cb}"))
+            nc.sync.dma_start(windows[cb][:], base[cb * P : (cb + 1) * P, :])
 
         identity = held.tile([P, P], F32, name="identity")
         masks.make_identity(nc, identity[:])
@@ -66,6 +60,8 @@ def tile_graphconvolutionlayer_kernel(tc, base, msg, h, w_i, w_h, b_i, b_hn, off
         nc.tensor.transpose(bias_ps[:], bias_rows[:], identity[:])
         bias = held.tile([P, 4 * BLOCKS], F32, name="bias")
         nc.vector.tensor_copy(bias[:], bias_ps[:, 0 : 4 * BLOCKS])
+        minus_bias = held.tile([P, 4 * BLOCKS], F32, name="minus_bias")
+        nc.vector.tensor_scalar_mul(minus_bias[:], bias_ps[:, 0 : 4 * BLOCKS], -1.0)
 
         def b_i_column(gate, cb):
             return bias[:, gate * BLOCKS + cb : gate * BLOCKS + cb + 1]
@@ -73,58 +69,49 @@ def tile_graphconvolutionlayer_kernel(tc, base, msg, h, w_i, w_h, b_i, b_hn, off
         def b_hn_column(cb):
             return bias[:, 3 * BLOCKS + cb : 3 * BLOCKS + cb + 1]
 
-        sum_r = [banks.tile([P, N], F32, name=f"sum_r{cb}", tag="bank") for cb in range(BLOCKS)]
-        sum_z = [banks.tile([P, N], F32, name=f"sum_z{cb}", tag="bank") for cb in range(BLOCKS)]
-        for kb in range(BLOCKS):
-            for w_sb, moving, first, last in ((w_i_rz[kb], msg_sb, kb == 0, False), (w_h_rz[kb], h_sb, False, kb == BLOCKS - 1)):
-                for gate, sums in ((RESET, sum_r), (UPDATE, sum_z)):
-                    for cb in range(BLOCKS):
-                        nc.tensor.matmul(
-                            sums[cb][:],
-                            lhsT=w_sb[:, gate * C + cb * P : gate * C + (cb + 1) * P],
-                            rhs=moving[:, kb, :],
-                            start=first,
-                            stop=last,
-                        )
-        r = held.tile([P, BLOCKS, N], F32, name="r")
-        z = held.tile([P, BLOCKS, N], F32, name="z")
-        for cb in range(BLOCKS):
-            nc.scalar.activation(r[:, cb, :], sum_r[cb][:], SIGMOID, bias=b_i_column(RESET, cb))
-        for cb in range(BLOCKS):
-            nc.scalar.activation(z[:, cb, :], sum_z[cb][:], SIGMOID, bias=b_i_column(UPDATE, cb))
-        kept = held.tile([P, BLOCKS, N], F32, name="kept")
-        nc.vector.tensor_tensor(kept[:], z[:], h_sb[:], MULT)
-        one_minus_z = held.tile([P, BLOCKS, N], F32, name="one_minus_z")
-        nc.vector.tensor_scalar(one_minus_z[:], z[:], -1.0, 1.0, op0=MULT, op1=ADD)
-
-        e_n = [banks.tile([P, N], F32, name=f"e_n{cb}", tag="bank") for cb in range(BLOCKS)]
-        for kb in range(BLOCKS):
+        def multiply(sums, w_sb, moving, kb, start, stop):
             for cb in range(BLOCKS):
                 nc.tensor.matmul(
-                    e_n[cb][:],
-                    lhsT=w_h_n[kb][:, cb * P : (cb + 1) * P],
-                    rhs=h_sb[:, kb, :],
-                    start=kb == 0,
-                    stop=kb == BLOCKS - 1,
+                    sums[cb][:], lhsT=w_sb[:, cb * P : (cb + 1) * P], rhs=moving[:, kb, :], start=start, stop=stop
                 )
-        gated = held.tile([P, BLOCKS, N], F32, name="gated")
-        for cb in range(BLOCKS):
-            nc.vector.scalar_tensor_tensor(gated[:, cb, :], e_n[cb][:], b_hn_column(cb), r[:, cb, :], op0=ADD, op1=MULT)
 
+        def new_sums(name):
+            return [banks.tile([P, N], F32, name=f"{name}{cb}", tag="bank") for cb in range(BLOCKS)]
+
+        LAST = BLOCKS - 1
+
+        sum_r = new_sums("sum_r")
+        for kb in range(BLOCKS):
+            multiply(sum_r, w_i_sb[RESET, kb], msg_sb, kb, start=kb == 0, stop=False)
+            multiply(sum_r, w_h_sb[RESET, kb], h_sb, kb, start=False, stop=kb == LAST)
+        r = held.tile([P, BLOCKS, N], F32, name="r")
         for cb in range(BLOCKS):
-            a_n = banks.tile([P, N], F32, name=f"a_n{cb}", tag="bank")
-            for kb in range(BLOCKS):
-                nc.tensor.matmul(
-                    a_n[:],
-                    lhsT=w_i_n[cb // 2][:, kb, (cb % 2) * P : (cb % 2 + 1) * P],
-                    rhs=msg_sb[:, kb, :],
-                    start=kb == 0,
-                    stop=kb == BLOCKS - 1,
-                )
-            n = held.tile([P, N], F32, name=f"n{cb}")
-            nc.vector.tensor_tensor(n[:], gated[:, cb, :], a_n[:], ADD)
-            nc.scalar.activation(n[:], n[:], TANH, bias=b_i_column(CANDIDATE, cb))
+            nc.scalar.activation(r[:, cb, :], sum_r[cb][:], SIGMOID, bias=b_i_column(RESET, cb))
+
+        e_n = new_sums("e_n")
+        a_n = new_sums("a_n")
+        for kb in range(BLOCKS):
+            multiply(e_n, w_h_sb[CANDIDATE, kb], h_sb, kb, start=kb == 0, stop=kb == LAST)
+            multiply(a_n, w_i_sb[CANDIDATE, kb], msg_sb, kb, start=kb == 0, stop=kb == LAST)
+        n = held.tile([P, BLOCKS, N], F32, name="n")
+        for cb in range(BLOCKS):
+            nc.vector.scalar_tensor_tensor(n[:, cb, :], e_n[cb][:], b_hn_column(cb), r[:, cb, :], op0=ADD, op1=MULT)
+            nc.vector.tensor_tensor(n[:, cb, :], n[:, cb, :], a_n[cb][:], ADD)
+            nc.scalar.activation(n[:, cb, :], n[:, cb, :], TANH, bias=b_i_column(CANDIDATE, cb))
+
+        sum_z = new_sums("sum_z")
+        for kb in range(BLOCKS):
+            multiply(sum_z, w_i_sb[UPDATE, kb], msg_sb, kb, start=kb == 0, stop=False)
+            multiply(sum_z, w_h_sb[UPDATE, kb], h_sb, kb, start=False, stop=kb == LAST)
+        for cb in range(BLOCKS):
+            z = held.tile([P, N], F32, name=f"z{cb}")
+            nc.scalar.activation(z[:], sum_z[cb][:], SIGMOID, bias=b_i_column(UPDATE, cb))
+            kept = held.tile([P, N], F32, name=f"kept{cb}")
+            nc.vector.tensor_tensor(kept[:], z[:], h_sb[:, cb, :], MULT)
+            one_minus_z = held.tile([P, N], F32, name=f"one_minus_z{cb}")
+            column = UPDATE * BLOCKS + cb
+            nc.scalar.activation(one_minus_z[:], sum_z[cb][:], SIGMOID, bias=minus_bias[:, column : column + 1], scale=-1.0)
             fresh = held.tile([P, N], F32, name=f"fresh{cb}")
-            nc.vector.tensor_tensor(fresh[:], one_minus_z[:, cb, :], n[:], MULT)
-            nc.vector.tensor_tensor(windows[cb][:].indirect(offsets[:]), fresh[:], kept[:, cb, :], ADD)
+            nc.vector.tensor_tensor(fresh[:], one_minus_z[:], n[:, cb, :], MULT)
+            nc.vector.tensor_tensor(windows[cb][:].indirect(offsets[:]), fresh[:], kept[:], ADD)
             nc.sync.dma_start(out[cb * P : (cb + 1) * P, :], windows[cb][:])

@@ -17,6 +17,8 @@ BLOCKS = C // P
 
 RESET, UPDATE, CANDIDATE = 0, 1, 2
 
+WARM_UP_MATMULS = 8
+
 FLOPS = 2 * 2 * C * 3 * C * N
 
 
@@ -53,6 +55,12 @@ def tile_graphconvolutionlayer_kernel(tc, base, msg, h, w_i, w_h, b_i, b_hn, off
         for cb in range(BLOCKS):
             windows.append(held.tile([P, S], F32, name=f"window{cb}"))
             nc.sync.dma_start(windows[cb][:], base[cb * P : (cb + 1) * P, :])
+
+        zeros = held.tile([P, 4 * P], BF16, name="zeros")
+        nc.vector.memset(zeros[:], 0.0)
+        idle_product = banks.tile([P, 4 * P], F32, name="idle_product", tag="bank")
+        for repeat in range(WARM_UP_MATMULS):
+            nc.tensor.matmul(idle_product[:], lhsT=zeros[:, 0:P], rhs=zeros[:], start=True, stop=True)
 
         identity = held.tile([P, P], F32, name="identity")
         masks.make_identity(nc, identity[:])

@@ -17,8 +17,6 @@ BLOCKS = C // P
 
 RESET, UPDATE, CANDIDATE = 0, 1, 2
 
-WARM_UP_MATMULS = 8
-
 FLOPS = 2 * 2 * C * 3 * C * N
 
 
@@ -28,10 +26,8 @@ def tile_graphconvolutionlayer_kernel(tc, base, msg, h, w_i, w_h, b_i, b_hn, off
         tc.tile_pool(name="held", bufs=1) as held,
         tc.psum_pool(name="banks", bufs=8) as banks,
     ):
-        offsets = held.tile([P, N // 16], U16, name="offsets")
-        nc.sync.dma_start(offsets[:], offs)
         msg_sb = held.tile([P, BLOCKS, N], BF16, name="msg_sb")
-        nc.sync.dma_start(msg_sb[:], msg.rearrange("(kb p) j -> p kb j", p=P))
+        nc.scalar.dma_start(msg_sb[:], msg.rearrange("(kb p) j -> p kb j", p=P))
         h_sb = held.tile([P, BLOCKS, N], BF16, name="h_sb")
         nc.scalar.dma_start(h_sb[:], h.rearrange("(kb p) j -> p kb j", p=P))
 
@@ -42,25 +38,36 @@ def tile_graphconvolutionlayer_kernel(tc, base, msg, h, w_i, w_h, b_i, b_hn, off
 
         w_i_sb = {}
         w_h_sb = {}
-        for gate in (RESET, CANDIDATE, UPDATE):
-            for kb in range(BLOCKS):
-                rows = slice(kb * P, (kb + 1) * P)
-                columns = slice(gate * C, (gate + 1) * C)
-                w_i_sb[gate, kb] = held.tile([P, C], BF16, name=f"w_i_sb{gate}_{kb}")
-                nc.sync.dma_start(w_i_sb[gate, kb][:], w_i[rows, columns])
-                w_h_sb[gate, kb] = held.tile([P, C], BF16, name=f"w_h_sb{gate}_{kb}")
-                nc.sync.dma_start(w_h_sb[gate, kb][:], w_h[rows, columns])
 
+        def load_w_i(gate, kb):
+            w_i_sb[gate, kb] = held.tile([P, C], BF16, name=f"w_i_sb{gate}_{kb}")
+            nc.sync.dma_start(w_i_sb[gate, kb][:], w_i[kb * P : (kb + 1) * P, gate * C : (gate + 1) * C])
+
+        def load_w_h(gate, kb):
+            w_h_sb[gate, kb] = held.tile([P, C], BF16, name=f"w_h_sb{gate}_{kb}")
+            nc.sync.dma_start(w_h_sb[gate, kb][:], w_h[kb * P : (kb + 1) * P, gate * C : (gate + 1) * C])
+
+        for kb in range(BLOCKS):
+            load_w_i(RESET, kb)
+            load_w_h(RESET, kb)
+        offsets = held.tile([P, N // 16], U16, name="offsets")
+        nc.sync.dma_start(offsets[:], offs)
+        w_h_n = held.tile([P, BLOCKS, C], BF16, name="w_h_n")
+        nc.sync.dma_start(w_h_n[:], w_h.rearrange("(kb p) m -> p kb m", p=P)[:, :, CANDIDATE * C : (CANDIDATE + 1) * C])
+        w_i_n = held.tile([P, BLOCKS, C], BF16, name="w_i_n")
+        nc.sync.dma_start(w_i_n[:], w_i.rearrange("(kb p) m -> p kb m", p=P)[:, :, CANDIDATE * C : (CANDIDATE + 1) * C])
+        w_i_z = []
+        w_h_z = []
         windows = []
-        for cb in range(BLOCKS):
-            windows.append(held.tile([P, S], F32, name=f"window{cb}"))
-            nc.sync.dma_start(windows[cb][:], base[cb * P : (cb + 1) * P, :])
-
-        zeros = held.tile([P, 4 * P], BF16, name="zeros")
-        nc.vector.memset(zeros[:], 0.0)
-        idle_product = banks.tile([P, 4 * P], F32, name="idle_product", tag="bank")
-        for repeat in range(WARM_UP_MATMULS):
-            nc.tensor.matmul(idle_product[:], lhsT=zeros[:, 0:P], rhs=zeros[:], start=True, stop=True)
+        for half in range(2):
+            columns = slice(UPDATE * C + half * 2 * P, UPDATE * C + (half + 1) * 2 * P)
+            w_i_z.append(held.tile([P, BLOCKS, 2 * P], BF16, name=f"w_i_z{half}"))
+            nc.sync.dma_start(w_i_z[half][:], w_i.rearrange("(kb p) m -> p kb m", p=P)[:, :, columns])
+            w_h_z.append(held.tile([P, BLOCKS, 2 * P], BF16, name=f"w_h_z{half}"))
+            nc.sync.dma_start(w_h_z[half][:], w_h.rearrange("(kb p) m -> p kb m", p=P)[:, :, columns])
+            for cb in (2 * half, 2 * half + 1):
+                windows.append(held.tile([P, S], F32, name=f"window{cb}"))
+                nc.sync.dma_start(windows[cb][:], base[cb * P : (cb + 1) * P, :])
 
         identity = held.tile([P, P], F32, name="identity")
         masks.make_identity(nc, identity[:])
@@ -96,29 +103,34 @@ def tile_graphconvolutionlayer_kernel(tc, base, msg, h, w_i, w_h, b_i, b_hn, off
         for cb in range(BLOCKS):
             nc.scalar.activation(r[:, cb, :], sum_r[cb][:], SIGMOID, bias=b_i_column(RESET, cb))
 
-        e_n = new_sums("e_n")
-        a_n = new_sums("a_n")
-        for kb in range(BLOCKS):
-            multiply(e_n, w_h_sb[CANDIDATE, kb], h_sb, kb, start=kb == 0, stop=kb == LAST)
-            multiply(a_n, w_i_sb[CANDIDATE, kb], msg_sb, kb, start=kb == 0, stop=kb == LAST)
         n = held.tile([P, BLOCKS, N], F32, name="n")
+        e_n = new_sums("e_n")
+        for kb in range(BLOCKS):
+            multiply(e_n, w_h_n[:, kb, :], h_sb, kb, start=kb == 0, stop=kb == LAST)
         for cb in range(BLOCKS):
             nc.vector.scalar_tensor_tensor(n[:, cb, :], e_n[cb][:], b_hn_column(cb), r[:, cb, :], op0=ADD, op1=MULT)
+        a_n = new_sums("a_n")
+        for kb in range(BLOCKS):
+            multiply(a_n, w_i_n[:, kb, :], msg_sb, kb, start=kb == 0, stop=kb == LAST)
+        for cb in range(BLOCKS):
             nc.vector.tensor_tensor(n[:, cb, :], n[:, cb, :], a_n[cb][:], ADD)
             nc.scalar.activation(n[:, cb, :], n[:, cb, :], TANH, bias=b_i_column(CANDIDATE, cb))
 
-        sum_z = new_sums("sum_z")
-        for kb in range(BLOCKS):
-            multiply(sum_z, w_i_sb[UPDATE, kb], msg_sb, kb, start=kb == 0, stop=False)
-            multiply(sum_z, w_h_sb[UPDATE, kb], h_sb, kb, start=False, stop=kb == LAST)
         for cb in range(BLOCKS):
+            half = cb // 2
+            block = slice((cb % 2) * P, (cb % 2 + 1) * P)
+            sum_z = banks.tile([P, N], F32, name=f"sum_z{cb}", tag="bank")
+            for kb in range(BLOCKS):
+                nc.tensor.matmul(sum_z[:], lhsT=w_i_z[half][:, kb, block], rhs=msg_sb[:, kb, :], start=kb == 0, stop=False)
+            for kb in range(BLOCKS):
+                nc.tensor.matmul(sum_z[:], lhsT=w_h_z[half][:, kb, block], rhs=h_sb[:, kb, :], start=False, stop=kb == LAST)
             z = held.tile([P, N], F32, name=f"z{cb}")
-            nc.scalar.activation(z[:], sum_z[cb][:], SIGMOID, bias=b_i_column(UPDATE, cb))
+            nc.scalar.activation(z[:], sum_z[:], SIGMOID, bias=b_i_column(UPDATE, cb))
             kept = held.tile([P, N], F32, name=f"kept{cb}")
             nc.vector.tensor_tensor(kept[:], z[:], h_sb[:, cb, :], MULT)
             one_minus_z = held.tile([P, N], F32, name=f"one_minus_z{cb}")
             column = UPDATE * BLOCKS + cb
-            nc.scalar.activation(one_minus_z[:], sum_z[cb][:], SIGMOID, bias=minus_bias[:, column : column + 1], scale=-1.0)
+            nc.scalar.activation(one_minus_z[:], sum_z[:], SIGMOID, bias=minus_bias[:, column : column + 1], scale=-1.0)
             fresh = held.tile([P, N], F32, name=f"fresh{cb}")
             nc.vector.tensor_tensor(fresh[:], one_minus_z[:], n[:, cb, :], MULT)
             nc.vector.tensor_tensor(windows[cb][:].indirect(offsets[:]), fresh[:], kept[:], ADD)

@@ -14,6 +14,8 @@ C = 512
 N = 128
 S = 256
 BLOCKS = C // P
+LAST = BLOCKS - 1
+EARLY = C + 2 * P
 
 RESET, UPDATE, CANDIDATE = 0, 1, 2
 
@@ -36,38 +38,28 @@ def tile_graphconvolutionlayer_kernel(tc, base, msg, h, w_i, w_h, b_i, b_hn, off
         nc.scalar.dma_start(bias_rows[0 : 3 * BLOCKS, :], b_i.rearrange("(n p) o -> n (p o)", p=P))
         nc.scalar.dma_start(bias_rows[3 * BLOCKS : 4 * BLOCKS, :], b_hn.rearrange("(n p) o -> n (p o)", p=P))
 
-        w_i_sb = {}
-        w_h_sb = {}
-
-        def load_w_i(gate, kb):
-            w_i_sb[gate, kb] = held.tile([P, C], BF16, name=f"w_i_sb{gate}_{kb}")
-            nc.sync.dma_start(w_i_sb[gate, kb][:], w_i[kb * P : (kb + 1) * P, gate * C : (gate + 1) * C])
-
-        def load_w_h(gate, kb):
-            w_h_sb[gate, kb] = held.tile([P, C], BF16, name=f"w_h_sb{gate}_{kb}")
-            nc.sync.dma_start(w_h_sb[gate, kb][:], w_h[kb * P : (kb + 1) * P, gate * C : (gate + 1) * C])
-
+        w_i_early = []
+        w_h_early = []
         for kb in range(BLOCKS):
-            load_w_i(RESET, kb)
-            load_w_h(RESET, kb)
+            w_i_early.append(held.tile([P, EARLY], BF16, name=f"w_i_early{kb}"))
+            nc.sync.dma_start(w_i_early[kb][:], w_i[kb * P : (kb + 1) * P, 0:EARLY])
+            w_h_early.append(held.tile([P, EARLY], BF16, name=f"w_h_early{kb}"))
+            nc.sync.dma_start(w_h_early[kb][:], w_h[kb * P : (kb + 1) * P, 0:EARLY])
         offsets = held.tile([P, N // 16], U16, name="offsets")
         nc.sync.dma_start(offsets[:], offs)
         w_h_n = held.tile([P, BLOCKS, C], BF16, name="w_h_n")
-        nc.sync.dma_start(w_h_n[:], w_h.rearrange("(kb p) m -> p kb m", p=P)[:, :, CANDIDATE * C : (CANDIDATE + 1) * C])
+        nc.sync.dma_start(w_h_n[:], w_h.rearrange("(kb p) m -> p kb m", p=P)[:, :, CANDIDATE * C : 3 * C])
         w_i_n = held.tile([P, BLOCKS, C], BF16, name="w_i_n")
-        nc.sync.dma_start(w_i_n[:], w_i.rearrange("(kb p) m -> p kb m", p=P)[:, :, CANDIDATE * C : (CANDIDATE + 1) * C])
-        w_i_z = []
-        w_h_z = []
-        windows = []
-        for half in range(2):
-            columns = slice(UPDATE * C + half * 2 * P, UPDATE * C + (half + 1) * 2 * P)
-            w_i_z.append(held.tile([P, BLOCKS, 2 * P], BF16, name=f"w_i_z{half}"))
-            nc.sync.dma_start(w_i_z[half][:], w_i.rearrange("(kb p) m -> p kb m", p=P)[:, :, columns])
-            w_h_z.append(held.tile([P, BLOCKS, 2 * P], BF16, name=f"w_h_z{half}"))
-            nc.sync.dma_start(w_h_z[half][:], w_h.rearrange("(kb p) m -> p kb m", p=P)[:, :, columns])
-            for cb in (2 * half, 2 * half + 1):
-                windows.append(held.tile([P, S], F32, name=f"window{cb}"))
-                nc.sync.dma_start(windows[cb][:], base[cb * P : (cb + 1) * P, :])
+        nc.sync.dma_start(w_i_n[:], w_i.rearrange("(kb p) m -> p kb m", p=P)[:, :, CANDIDATE * C : 3 * C])
+        windows = [held.tile([P, S], F32, name=f"window{cb}") for cb in range(BLOCKS)]
+        for cb in (0, 1):
+            nc.sync.dma_start(windows[cb][:], base[cb * P : (cb + 1) * P, :])
+        w_i_late = held.tile([P, BLOCKS, 2 * P], BF16, name="w_i_late")
+        nc.sync.dma_start(w_i_late[:], w_i.rearrange("(kb p) m -> p kb m", p=P)[:, :, EARLY : 2 * C])
+        w_h_late = held.tile([P, BLOCKS, 2 * P], BF16, name="w_h_late")
+        nc.sync.dma_start(w_h_late[:], w_h.rearrange("(kb p) m -> p kb m", p=P)[:, :, EARLY : 2 * C])
+        for cb in (2, 3):
+            nc.sync.dma_start(windows[cb][:], base[cb * P : (cb + 1) * P, :])
 
         identity = held.tile([P, P], F32, name="identity")
         masks.make_identity(nc, identity[:])
@@ -78,60 +70,65 @@ def tile_graphconvolutionlayer_kernel(tc, base, msg, h, w_i, w_h, b_i, b_hn, off
         minus_bias = held.tile([P, 4 * BLOCKS], F32, name="minus_bias")
         nc.vector.tensor_scalar_mul(minus_bias[:], bias_ps[:, 0 : 4 * BLOCKS], -1.0)
 
-        def b_i_column(gate, cb):
-            return bias[:, gate * BLOCKS + cb : gate * BLOCKS + cb + 1]
+        def column(biases, row):
+            return biases[:, row : row + 1]
 
-        def b_hn_column(cb):
-            return bias[:, 3 * BLOCKS + cb : 3 * BLOCKS + cb + 1]
+        def new_bank(name):
+            return banks.tile([P, N], F32, name=name, tag="bank")
 
-        def multiply(sums, w_sb, moving, kb, start, stop):
-            for cb in range(BLOCKS):
-                nc.tensor.matmul(
-                    sums[cb][:], lhsT=w_sb[:, cb * P : (cb + 1) * P], rhs=moving[:, kb, :], start=start, stop=stop
-                )
-
-        def new_sums(name):
-            return [banks.tile([P, N], F32, name=f"{name}{cb}", tag="bank") for cb in range(BLOCKS)]
-
-        LAST = BLOCKS - 1
-
-        sum_r = new_sums("sum_r")
-        for kb in range(BLOCKS):
-            multiply(sum_r, w_i_sb[RESET, kb], msg_sb, kb, start=kb == 0, stop=False)
-            multiply(sum_r, w_h_sb[RESET, kb], h_sb, kb, start=False, stop=kb == LAST)
         r = held.tile([P, BLOCKS, N], F32, name="r")
-        for cb in range(BLOCKS):
-            nc.scalar.activation(r[:, cb, :], sum_r[cb][:], SIGMOID, bias=b_i_column(RESET, cb))
-
         n = held.tile([P, BLOCKS, N], F32, name="n")
-        e_n = new_sums("e_n")
+        one_minus_z = held.tile([P, BLOCKS, N], F32, name="one_minus_z")
+        kept = held.tile([P, BLOCKS, N], F32, name="kept")
+
+        def update_gate(cb, sum_z):
+            z = held.tile([P, N], F32, name=f"z{cb}")
+            nc.scalar.activation(z[:], sum_z[:], SIGMOID, bias=column(bias, UPDATE * BLOCKS + cb))
+            nc.scalar.activation(
+                one_minus_z[:, cb, :], sum_z[:], SIGMOID, bias=column(minus_bias, UPDATE * BLOCKS + cb), scale=-1.0
+            )
+            nc.vector.tensor_tensor(kept[:, cb, :], z[:], h_sb[:, cb, :], MULT)
+
+        def scatter(cb):
+            fresh = held.tile([P, N], F32, name=f"fresh{cb}")
+            nc.vector.tensor_tensor(fresh[:], one_minus_z[:, cb, :], n[:, cb, :], MULT)
+            nc.vector.tensor_tensor(windows[cb][:].indirect(offsets[:]), fresh[:], kept[:, cb, :], ADD)
+            nc.sync.dma_start(out[cb * P : (cb + 1) * P, :], windows[cb][:])
+
+        early_sums = [new_bank(f"early_sum{i}") for i in range(EARLY // P)]
         for kb in range(BLOCKS):
-            multiply(e_n, w_h_n[:, kb, :], h_sb, kb, start=kb == 0, stop=kb == LAST)
+            for i in range(EARLY // P):
+                nc.tensor.matmul(
+                    early_sums[i][:], lhsT=w_i_early[kb][:, i * P : (i + 1) * P], rhs=msg_sb[:, kb, :], start=kb == 0, stop=False
+                )
+            for i in range(EARLY // P):
+                nc.tensor.matmul(
+                    early_sums[i][:], lhsT=w_h_early[kb][:, i * P : (i + 1) * P], rhs=h_sb[:, kb, :], start=False, stop=kb == LAST
+                )
         for cb in range(BLOCKS):
-            nc.vector.scalar_tensor_tensor(n[:, cb, :], e_n[cb][:], b_hn_column(cb), r[:, cb, :], op0=ADD, op1=MULT)
-        a_n = new_sums("a_n")
-        for kb in range(BLOCKS):
-            multiply(a_n, w_i_n[:, kb, :], msg_sb, kb, start=kb == 0, stop=kb == LAST)
-        for cb in range(BLOCKS):
-            nc.vector.tensor_tensor(n[:, cb, :], n[:, cb, :], a_n[cb][:], ADD)
-            nc.scalar.activation(n[:, cb, :], n[:, cb, :], TANH, bias=b_i_column(CANDIDATE, cb))
+            nc.scalar.activation(r[:, cb, :], early_sums[cb][:], SIGMOID, bias=column(bias, RESET * BLOCKS + cb))
+        for cb in (0, 1):
+            update_gate(cb, early_sums[BLOCKS + cb])
 
         for cb in range(BLOCKS):
-            half = cb // 2
-            block = slice((cb % 2) * P, (cb % 2 + 1) * P)
-            sum_z = banks.tile([P, N], F32, name=f"sum_z{cb}", tag="bank")
+            e_n = new_bank(f"e_n{cb}")
             for kb in range(BLOCKS):
-                nc.tensor.matmul(sum_z[:], lhsT=w_i_z[half][:, kb, block], rhs=msg_sb[:, kb, :], start=kb == 0, stop=False)
+                nc.tensor.matmul(e_n[:], lhsT=w_h_n[:, kb, cb * P : (cb + 1) * P], rhs=h_sb[:, kb, :], start=kb == 0, stop=kb == LAST)
+            nc.vector.scalar_tensor_tensor(n[:, cb, :], e_n[:], column(bias, 3 * BLOCKS + cb), r[:, cb, :], op0=ADD, op1=MULT)
+        for cb in range(BLOCKS):
+            a_n = new_bank(f"a_n{cb}")
             for kb in range(BLOCKS):
-                nc.tensor.matmul(sum_z[:], lhsT=w_h_z[half][:, kb, block], rhs=h_sb[:, kb, :], start=False, stop=kb == LAST)
-            z = held.tile([P, N], F32, name=f"z{cb}")
-            nc.scalar.activation(z[:], sum_z[:], SIGMOID, bias=b_i_column(UPDATE, cb))
-            kept = held.tile([P, N], F32, name=f"kept{cb}")
-            nc.vector.tensor_tensor(kept[:], z[:], h_sb[:, cb, :], MULT)
-            one_minus_z = held.tile([P, N], F32, name=f"one_minus_z{cb}")
-            column = UPDATE * BLOCKS + cb
-            nc.scalar.activation(one_minus_z[:], sum_z[:], SIGMOID, bias=minus_bias[:, column : column + 1], scale=-1.0)
-            fresh = held.tile([P, N], F32, name=f"fresh{cb}")
-            nc.vector.tensor_tensor(fresh[:], one_minus_z[:], n[:, cb, :], MULT)
-            nc.vector.tensor_tensor(windows[cb][:].indirect(offsets[:]), fresh[:], kept[:], ADD)
-            nc.sync.dma_start(out[cb * P : (cb + 1) * P, :], windows[cb][:])
+                nc.tensor.matmul(a_n[:], lhsT=w_i_n[:, kb, cb * P : (cb + 1) * P], rhs=msg_sb[:, kb, :], start=kb == 0, stop=kb == LAST)
+            nc.vector.tensor_tensor(n[:, cb, :], n[:, cb, :], a_n[:], ADD)
+            nc.scalar.activation(n[:, cb, :], n[:, cb, :], TANH, bias=column(bias, CANDIDATE * BLOCKS + cb))
+
+        for cb in (0, 1):
+            scatter(cb)
+        for cb in (2, 3):
+            sum_z = new_bank(f"sum_z{cb}")
+            for kb in range(BLOCKS):
+                nc.tensor.matmul(sum_z[:], lhsT=w_i_late[:, kb, (cb - 2) * P : (cb - 1) * P], rhs=msg_sb[:, kb, :], start=kb == 0, stop=False)
+            for kb in range(BLOCKS):
+                nc.tensor.matmul(sum_z[:], lhsT=w_h_late[:, kb, (cb - 2) * P : (cb - 1) * P], rhs=h_sb[:, kb, :], start=False, stop=kb == LAST)
+            update_gate(cb, sum_z)
+            scatter(cb)

@@ -61,15 +61,6 @@ def tile_graphconvolutionlayer_kernel(tc, base, msg, h, w_i, w_h, b_i, b_hn, off
         for cb in (2, 3):
             nc.sync.dma_start(windows[cb][:], base[cb * P : (cb + 1) * P, :])
 
-        identity = held.tile([P, P], F32, name="identity")
-        masks.make_identity(nc, identity[:])
-        bias_ps = banks.tile([P, P], F32, name="bias_ps", tag="bank")
-        nc.tensor.transpose(bias_ps[:], bias_rows[:], identity[:])
-        bias = held.tile([P, 4 * BLOCKS], F32, name="bias")
-        nc.vector.tensor_copy(bias[:], bias_ps[:, 0 : 4 * BLOCKS])
-        minus_bias = held.tile([P, 4 * BLOCKS], F32, name="minus_bias")
-        nc.vector.tensor_scalar_mul(minus_bias[:], bias_ps[:, 0 : 4 * BLOCKS], -1.0)
-
         def column(biases, row):
             return biases[:, row : row + 1]
 
@@ -105,6 +96,15 @@ def tile_graphconvolutionlayer_kernel(tc, base, msg, h, w_i, w_h, b_i, b_hn, off
                 nc.tensor.matmul(
                     early_sums[i][:], lhsT=w_h_early[kb][:, i * P : (i + 1) * P], rhs=h_sb[:, kb, :], start=False, stop=kb == LAST
                 )
+        identity = held.tile([P, P], F32, name="identity")
+        masks.make_identity(nc, identity[:])
+        bias_ps = banks.tile([P, P], F32, name="bias_ps", tag="bank")
+        nc.tensor.transpose(bias_ps[:], bias_rows[:], identity[:])
+        bias = held.tile([P, 4 * BLOCKS], F32, name="bias")
+        nc.vector.tensor_copy(bias[:], bias_ps[:, 0 : 4 * BLOCKS])
+        minus_bias = held.tile([P, 4 * BLOCKS], F32, name="minus_bias")
+        nc.vector.tensor_scalar_mul(minus_bias[:], bias_ps[:, 0 : 4 * BLOCKS], -1.0)
+
         for cb in range(BLOCKS):
             nc.scalar.activation(r[:, cb, :], early_sums[cb][:], SIGMOID, bias=column(bias, RESET * BLOCKS + cb))
         for cb in (0, 1):

@@ -29,7 +29,8 @@ def tile_graphconvolutionlayer_kernel(tc, base, msg, h, w_i, w_h, b_i, b_hn, off
         tc.psum_pool(name="banks", bufs=8) as banks,
     ):
         msg_sb = held.tile([P, BLOCKS, N], BF16, name="msg_sb")
-        nc.scalar.dma_start(msg_sb[:], msg.rearrange("(kb p) j -> p kb j", p=P))
+        nc.scalar.dma_start(msg_sb[:], msg.rearrange("(p kb) j -> p kb j", kb=BLOCKS))
+        w_i_blocks = w_i.rearrange("(p kb) m -> p kb m", kb=BLOCKS)
         h_sb = held.tile([P, BLOCKS, N], BF16, name="h_sb")
         nc.scalar.dma_start(h_sb[:], h.rearrange("(kb p) j -> p kb j", p=P))
 
@@ -42,20 +43,20 @@ def tile_graphconvolutionlayer_kernel(tc, base, msg, h, w_i, w_h, b_i, b_hn, off
         w_h_early = []
         for kb in range(BLOCKS):
             w_i_early.append(held.tile([P, EARLY], BF16, name=f"w_i_early{kb}"))
-            nc.sync.dma_start(w_i_early[kb][:], w_i[kb * P : (kb + 1) * P, 0:EARLY])
+            nc.sync.dma_start(w_i_early[kb][:], w_i_blocks[:, kb, 0:EARLY])
             w_h_early.append(held.tile([P, EARLY], BF16, name=f"w_h_early{kb}"))
             nc.sync.dma_start(w_h_early[kb][:], w_h[kb * P : (kb + 1) * P, 0:EARLY])
-        offsets = held.tile([P, N // 16], U16, name="offsets")
-        nc.sync.dma_start(offsets[:], offs)
         w_h_n = held.tile([P, BLOCKS, C], BF16, name="w_h_n")
         nc.sync.dma_start(w_h_n[:], w_h.rearrange("(kb p) m -> p kb m", p=P)[:, :, CANDIDATE * C : 3 * C])
         w_i_n = held.tile([P, BLOCKS, C], BF16, name="w_i_n")
-        nc.sync.dma_start(w_i_n[:], w_i.rearrange("(kb p) m -> p kb m", p=P)[:, :, CANDIDATE * C : 3 * C])
+        nc.sync.dma_start(w_i_n[:], w_i_blocks[:, :, CANDIDATE * C : 3 * C])
+        offsets = held.tile([P, N // 16], U16, name="offsets")
+        nc.sync.dma_start(offsets[:], offs)
         windows = [held.tile([P, S], F32, name=f"window{cb}") for cb in range(BLOCKS)]
         for cb in (0, 1):
             nc.sync.dma_start(windows[cb][:], base[cb * P : (cb + 1) * P, :])
         w_i_late = held.tile([P, BLOCKS, 2 * P], BF16, name="w_i_late")
-        nc.sync.dma_start(w_i_late[:], w_i.rearrange("(kb p) m -> p kb m", p=P)[:, :, EARLY : 2 * C])
+        nc.sync.dma_start(w_i_late[:], w_i_blocks[:, :, EARLY : 2 * C])
         w_h_late = held.tile([P, BLOCKS, 2 * P], BF16, name="w_h_late")
         nc.sync.dma_start(w_h_late[:], w_h.rearrange("(kb p) m -> p kb m", p=P)[:, :, EARLY : 2 * C])
         for cb in (2, 3):

import concourse.masks as masks
import concourse.mybir as mybir

F32 = mybir.dt.float32
BF16 = mybir.dt.bfloat16
U16 = mybir.dt.uint16
ADD = mybir.AluOpType.add
MULT = mybir.AluOpType.mult
SIGMOID = mybir.ActivationFunctionType.Sigmoid
TANH = mybir.ActivationFunctionType.Tanh

P = 128
C = 512
N = 128
S = 256
BLOCKS = C // P
LAST = BLOCKS - 1
EARLY = C + 2 * P

RESET, UPDATE, CANDIDATE = 0, 1, 2

FLOPS = 2 * 2 * C * 3 * C * N


def tile_graphconvolutionlayer_kernel(tc, base, msg, h, w_i, w_h, b_i, b_hn, offs, out):
    nc = tc.nc
    with (
        tc.tile_pool(name="held", bufs=1) as held,
        tc.psum_pool(name="banks", bufs=8) as banks,
    ):
        msg_sb = held.tile([P, BLOCKS, N], BF16, name="msg_sb")
        nc.scalar.dma_start(msg_sb[:], msg.rearrange("(p kb) j -> p kb j", kb=BLOCKS))
        w_i_blocks = w_i.rearrange("(p kb) m -> p kb m", kb=BLOCKS)
        h_sb = held.tile([P, BLOCKS, N], BF16, name="h_sb")
        nc.scalar.dma_start(h_sb[:], h.rearrange("(kb p) j -> p kb j", p=P))

        bias_rows = held.tile([P, P], F32, name="bias_rows")
        nc.vector.memset(bias_rows[:], 0.0)
        nc.scalar.dma_start(bias_rows[0 : 3 * BLOCKS, :], b_i.rearrange("(n p) o -> n (p o)", p=P))
        nc.scalar.dma_start(bias_rows[3 * BLOCKS : 4 * BLOCKS, :], b_hn.rearrange("(n p) o -> n (p o)", p=P))

        w_i_early = []
        w_h_early = []
        for kb in range(BLOCKS):
            w_i_early.append(held.tile([P, EARLY], BF16, name=f"w_i_early{kb}"))
            nc.sync.dma_start(w_i_early[kb][:], w_i_blocks[:, kb, 0:EARLY])
            w_h_early.append(held.tile([P, EARLY], BF16, name=f"w_h_early{kb}"))
            nc.sync.dma_start(w_h_early[kb][:], w_h[kb * P : (kb + 1) * P, 0:EARLY])
        w_h_n = held.tile([P, BLOCKS, C], BF16, name="w_h_n")
        nc.sync.dma_start(w_h_n[:], w_h.rearrange("(kb p) m -> p kb m", p=P)[:, :, CANDIDATE * C : 3 * C])
        w_i_n = held.tile([P, BLOCKS, C], BF16, name="w_i_n")
        nc.sync.dma_start(w_i_n[:], w_i_blocks[:, :, CANDIDATE * C : 3 * C])
        offsets = held.tile([P, N // 16], U16, name="offsets")
        nc.sync.dma_start(offsets[:], offs)
        windows = [held.tile([P, S], F32, name=f"window{cb}") for cb in range(BLOCKS)]
        for cb in (0, 1):
            nc.sync.dma_start(windows[cb][:], base[cb * P : (cb + 1) * P, :])
        w_i_late = held.tile([P, BLOCKS, 2 * P], BF16, name="w_i_late")
        nc.sync.dma_start(w_i_late[:], w_i_blocks[:, :, EARLY : 2 * C])
        w_h_late = held.tile([P, BLOCKS, 2 * P], BF16, name="w_h_late")
        nc.sync.dma_start(w_h_late[:], w_h.rearrange("(kb p) m -> p kb m", p=P)[:, :, EARLY : 2 * C])
        for cb in (2, 3):
            nc.sync.dma_start(windows[cb][:], base[cb * P : (cb + 1) * P, :])

        def column(biases, row):
            return biases[:, row : row + 1]

        def new_bank(name):
            return banks.tile([P, N], F32, name=name, tag="bank")

        r = held.tile([P, BLOCKS, N], F32, name="r")
        n = held.tile([P, BLOCKS, N], F32, name="n")
        one_minus_z = held.tile([P, BLOCKS, N], F32, name="one_minus_z")
        kept = held.tile([P, BLOCKS, N], F32, name="kept")

        def update_gate(cb, sum_z):
            z = held.tile([P, N], F32, name=f"z{cb}")
            nc.scalar.activation(z[:], sum_z[:], SIGMOID, bias=column(bias, UPDATE * BLOCKS + cb))
            nc.scalar.activation(
                one_minus_z[:, cb, :], sum_z[:], SIGMOID, bias=column(minus_bias, UPDATE * BLOCKS + cb), scale=-1.0
            )
            nc.vector.tensor_tensor(kept[:, cb, :], z[:], h_sb[:, cb, :], MULT)

        def scatter(cb):
            fresh = held.tile([P, N], F32, name=f"fresh{cb}")
            nc.vector.tensor_tensor(fresh[:], one_minus_z[:, cb, :], n[:, cb, :], MULT)
            nc.vector.tensor_tensor(windows[cb][:].indirect(offsets[:]), fresh[:], kept[:, cb, :], ADD)
            nc.sync.dma_start(out[cb * P : (cb + 1) * P, :], windows[cb][:])

        early_sums = [new_bank(f"early_sum{i}") for i in range(EARLY // P)]
        for kb in range(BLOCKS):
            for i in range(EARLY // P):
                nc.tensor.matmul(
                    early_sums[i][:], lhsT=w_i_early[kb][:, i * P : (i + 1) * P], rhs=msg_sb[:, kb, :], start=kb == 0, stop=False
                )
            for i in range(EARLY // P):
                nc.tensor.matmul(
                    early_sums[i][:], lhsT=w_h_early[kb][:, i * P : (i + 1) * P], rhs=h_sb[:, kb, :], start=False, stop=kb == LAST
                )
        identity = held.tile([P, P], F32, name="identity")
        masks.make_identity(nc, identity[:])
        bias_ps = banks.tile([P, P], F32, name="bias_ps", tag="bank")
        nc.tensor.transpose(bias_ps[:], bias_rows[:], identity[:])
        bias = held.tile([P, 4 * BLOCKS], F32, name="bias")
        nc.vector.tensor_copy(bias[:], bias_ps[:, 0 : 4 * BLOCKS])
        minus_bias = held.tile([P, 4 * BLOCKS], F32, name="minus_bias")
        nc.vector.tensor_scalar_mul(minus_bias[:], bias_ps[:, 0 : 4 * BLOCKS], -1.0)

        for cb in range(BLOCKS):
            nc.scalar.activation(r[:, cb, :], early_sums[cb][:], SIGMOID, bias=column(bias, RESET * BLOCKS + cb))
        for cb in (0, 1):
            update_gate(cb, early_sums[BLOCKS + cb])

        for cb in range(BLOCKS):
            e_n = new_bank(f"e_n{cb}")
            for kb in range(BLOCKS):
                nc.tensor.matmul(e_n[:], lhsT=w_h_n[:, kb, cb * P : (cb + 1) * P], rhs=h_sb[:, kb, :], start=kb == 0, stop=kb == LAST)
            nc.vector.scalar_tensor_tensor(n[:, cb, :], e_n[:], column(bias, 3 * BLOCKS + cb), r[:, cb, :], op0=ADD, op1=MULT)
        for cb in range(BLOCKS):
            a_n = new_bank(f"a_n{cb}")
            for kb in range(BLOCKS):
                nc.tensor.matmul(a_n[:], lhsT=w_i_n[:, kb, cb * P : (cb + 1) * P], rhs=msg_sb[:, kb, :], start=kb == 0, stop=kb == LAST)
            nc.vector.tensor_tensor(n[:, cb, :], n[:, cb, :], a_n[:], ADD)
            nc.scalar.activation(n[:, cb, :], n[:, cb, :], TANH, bias=column(bias, CANDIDATE * BLOCKS + cb))

        for cb in (0, 1):
            scatter(cb)
        for cb in (2, 3):
            sum_z = new_bank(f"sum_z{cb}")
            for kb in range(BLOCKS):
                nc.tensor.matmul(sum_z[:], lhsT=w_i_late[:, kb, (cb - 2) * P : (cb - 1) * P], rhs=msg_sb[:, kb, :], start=kb == 0, stop=False)
            for kb in range(BLOCKS):
                nc.tensor.matmul(sum_z[:], lhsT=w_h_late[:, kb, (cb - 2) * P : (cb - 1) * P], rhs=h_sb[:, kb, :], start=False, stop=kb == LAST)
            update_gate(cb, sum_z)
            scatter(cb)
